import numpy as np
import ml_dtypes


def mxq(x, axis, fmt="e4m3"):
    dtype, down = {"e4m3": (ml_dtypes.float8_e4m3fn, 7), "e5m2": (ml_dtypes.float8_e5m2, 14)}[fmt]
    v = np.moveaxis(np.asarray(x, np.float32).astype(ml_dtypes.bfloat16).astype(np.float64), axis, -1)
    blocks = v.reshape(v.shape[:-1] + (-1, 32))
    amax = np.abs(blocks).max(-1, keepdims=True)
    byte = np.maximum(np.where(amax > 0, np.frexp(amax)[1] - 1 + 127, 0) - down, 1)
    scale = np.exp2(byte - 127.0)
    codes = (blocks / scale).astype(np.float32).astype(dtype).astype(np.float64)
    return np.moveaxis((codes * scale).reshape(v.shape), -1, axis)


WIDE = False


def mx_kscale(k):
    if not WIDE:
        return np.ones(k)
    levels = np.array([18, -18])
    if k % 512:
        return np.exp2(np.random.permutation(np.resize(levels, k // 32))).repeat(32)
    a = np.empty((k // 512, 16))
    for p in range(k // 512):
        a[p, :8] = np.random.permutation(np.resize(levels, 8))
        for g in range(8):
            far = levels[np.abs(levels - a[p, g]) >= 10]
            a[p, g + 8] = far[np.random.randint(len(far))]
    return np.exp2(a.ravel()).repeat(32)


BF16 = ml_dtypes.bfloat16


def bf(x):
    return np.asarray(x, np.float32).astype(BF16)


def f64(x):
    return np.asarray(x).astype(np.float64)


B, S, D, H, HD = 1, 512, 1024, 8, 128
T = B * S
J = H * HD
EPS = 1e-5
THETA = 10000.0


def inv_rms_of(x):
    return 1.0 / np.sqrt(np.mean(x * x, axis=-1, keepdims=True) + EPS)


def rope_tables(s, hd):
    inv_freq = 1.0 / (THETA ** (f64(np.arange(0, hd, 2)) / hd))
    ang = f64(np.arange(s))[:, None] * inv_freq[None, :]
    return np.cos(ang)[None, :, None, :], np.sin(ang)[None, :, None, :]


def rope_back(g):
    cos, sin = rope_tables(g.shape[1], g.shape[-1])
    g1 = g[..., 0::2]
    g2 = g[..., 1::2]
    d1 = g1 * cos + g2 * sin
    d2 = g2 * cos - g1 * sin
    return np.stack([d1, d2], axis=-1).reshape(g.shape)


def setup_inputs():
    s = mx_kscale(T)
    uq = mx_kscale(J)
    uk = mx_kscale(J)
    uv = mx_kscale(J)
    c = 1.0 / np.sqrt(D)
    x0 = bf(np.random.standard_normal((B, S, D)))
    ln_w = bf(1.0 + 0.1 * np.random.standard_normal(D))
    wq0 = bf(np.random.standard_normal((D, J)) * c)
    wk0 = bf(np.random.standard_normal((D, J)) * c)
    wv0 = bf(np.random.standard_normal((D, J)) * c)
    inv_rms = inv_rms_of(f64(x0))
    st = s.reshape(B, S, 1)

    def grad(u):
        n = np.random.standard_normal((B, S, H, HD))
        e = np.exp2(np.random.randint(-6, 1, (B, S, 1, 1)))
        return bf(n * e / st[..., None] * u.reshape(H, HD))

    return {"x": bf(f64(x0) * st),
            "ln_w": ln_w,
            "wq": bf(f64(wq0) / uq),
            "wk": bf(f64(wk0) / uk),
            "wv": bf(f64(wv0) / uv),
            "inv_rms": np.asarray(inv_rms, np.float32),
            "grad_0": grad(uq),
            "grad_1": grad(uk),
            "grad_2": grad(uv)}


def reference(x, ln_w, wq, wk, wv, inv_rms, grad_0, grad_1, grad_2):
    iv = f64(inv_rms).reshape(T, 1)
    lw = f64(ln_w)
    xh = f64(x).reshape(T, D) * iv
    xn = xh * lw
    dzq = rope_back(f64(grad_0)).reshape(T, J)
    dzk = rope_back(f64(grad_1)).reshape(T, J)
    dzv = f64(grad_2).reshape(T, J)
    dz = np.concatenate([dzq, dzk, dzv], axis=1)
    w = np.concatenate([f64(wq), f64(wk), f64(wv)], axis=1)
    dxn = mxq(dz, 1, "e5m2") @ mxq(w, 1, "e4m3").T
    dw = mxq(xn, 0, "e4m3").T @ mxq(dz, 0, "e5m2")
    g = dxn * lw
    dx = iv * (g - xh * np.mean(g * xh, axis=1, keepdims=True))
    return dx.reshape(B, S, D), dw[:, :J], dw[:, J:2 * J], dw[:, 2 * J:]

@@ -1,0 +1,508 @@
+import math
+from contextlib import ExitStack
+
+import concourse.mybir as mybir
+from concourse.masks import make_identity
+
+T, D, J = 512, 1024, 1024
+HD = 128
+THETA = 10000.0
+FLOPS = 2 * 2 * T * D * 3 * J
+
+F32 = mybir.dt.float32
+BF16 = mybir.dt.bfloat16
+I32 = mybir.dt.int32
+U32 = mybir.dt.uint32
+U8 = mybir.dt.uint8
+E4 = mybir.dt.float8_e4m3fn_x4
+E5 = mybir.dt.float8_e5m2_x4
+ALU = mybir.AluOpType
+ACT = mybir.ActivationFunctionType
+
+P = 128
+R = 4
+N = 512
+ORDER = (0, 1, 4, 5, 2, 3)
+
+
+def tile_pagedllamablock_pa_v_kernel(tc, x, ln_w, wq, wk, wv, inv_rms, grad_0, grad_1, grad_2, out_0, out_1, out_2, out_3):
+    nc = tc.nc
+    weights = (wq, wk, wv)
+    grads = (grad_0, grad_1, grad_2)
+    dw_out = (out_1, out_2, out_3)
+
+    with ExitStack() as ctx:
+        keep = ctx.enter_context(tc.tile_pool(name="keep", bufs=1))
+        ring = ctx.enter_context(tc.tile_pool(name="ring", bufs=1))
+        psum = ctx.enter_context(tc.psum_pool(name="psum", bufs=1))
+        ctx.enter_context(tc.manual_schedule())
+
+        def turn_bank(name):
+            return psum.tile([P, N], F32, name=name, tag="turn", bufs=4)
+
+        def sum_bank(name):
+            return psum.tile([P, N], F32, name=name, tag="sum", bufs=4)
+
+        def staged(name):
+            return ring.tile([P, N * R], BF16, name=name, tag="staged", bufs=7, align_bytes=64)
+
+        def operand(name, width):
+            codes = keep.tile([P, width], U32, name=name + "_codes", align_bytes=64)
+            scales = keep.tile([P, width], U8, name=name + "_scales", align_bytes=64)
+            return codes, scales
+
+        iv = keep.tile([P, R], F32, name="iv")
+        lw_cols = keep.tile([P, 2, R], BF16, name="lw_cols")
+        x_sb = keep.tile([P, R, D], BF16, name="x_sb")
+        g_sb = [keep.tile([P, R, N], BF16, name="g%d" % g) for g in range(6)]
+        w_sb = {(i, h): keep.tile([P, R, J], BF16, name="w%d%d" % (i, h)) for i in range(3) for h in range(2)}
+
+        def load_g(g):
+            rows = grads[g // 2].rearrange("b (p j) h e -> p (b j) (h e)", j=R)
+            nc.sync.dma_start(out=g_sb[g][:], in_=rows[:, :, (g % 2) * N:(g % 2 + 1) * N])
+
+        def load_x(h):
+            rows = x.rearrange("b (p j) d -> p (b j) d", j=R)
+            nc.sync.dma_start(out=x_sb[:, :, h * N:(h + 1) * N], in_=rows[:, :, h * N:(h + 1) * N])
+
+        def load_w(i, h):
+            nc.sync.dma_start(out=w_sb[i, h][:], in_=weights[i][h * N:(h + 1) * N, :].rearrange("(p b) c -> p b c", b=R))
+
+        nc.sync.dma_start(out=lw_cols[:], in_=ln_w.rearrange("(h p b) -> p h b", h=2, b=R))
+        nc.sync.dma_start(out=iv[:], in_=inv_rms.rearrange("b (p j) o -> p (b j o)", j=R))
+        load_g(4)
+        load_x(0)
+        load_g(0)
+        load_g(5)
+        load_g(1)
+        load_x(1)
+        load_w(0, 0)
+        load_w(2, 0)
+        load_g(2)
+        load_w(1, 0)
+        load_g(3)
+        for i in range(3):
+            load_w(i, 1)
+
+        pos = keep.tile([P, R], I32, name="pos")
+        nc.gpsimd.iota(pos[:], pattern=[[1, R]], base=0, channel_multiplier=R)
+        ident = keep.tile([P, P], F32, name="ident")
+        make_identity(nc, ident[:])
+
+        turns = keep.tile([P, R, 8, 8], F32, name="turns")
+        for u in range(2):
+            for mi in range(4):
+                nc.vector.tensor_scalar(out=turns[:, :, 0, 4 * u + mi], in0=pos[:], scalar1=THETA ** (-(2 * mi + u) / 64) / (2 * math.pi), scalar2=None, op0=ALU.mult)
+        for mm in range(1, 8):
+            nc.vector.tensor_scalar(out=turns[:, :, mm, :], in0=turns[:, :, 0, :], scalar1=THETA ** (-mm / 8), scalar2=None, op0=ALU.mult)
+        flat = turns[:].rearrange("p j a b -> p (j a b)")
+        whole = keep.tile([P, 256], I32, name="whole")
+        nc.vector.tensor_copy(out=whole[:], in_=flat)
+        lw_f32 = keep.tile([P, 2, R], F32, name="lw_f32")
+        nc.vector.tensor_copy(out=lw_f32[:], in_=lw_cols[:])
+        frac = keep.tile([P, 256], F32, name="frac")
+        nc.vector.tensor_tensor(out=frac[:], in0=flat, in1=whole[:], op=ALU.subtract)
+        mean_coef = keep.tile([P, R], F32, name="mean_coef")
+        nc.vector.scalar_tensor_tensor(out=mean_coef[:], in0=iv[:], scalar=-1.0 / D, in1=iv[:], op0=ALU.mult, op1=ALU.mult)
+        quarter = keep.tile([P, 256], F32, name="quarter")
+        nc.vector.scalar_tensor_tensor(out=quarter[:], in0=frac[:], scalar=-1.0, in1=frac[:], op0=ALU.mult, op1=ALU.min)
+        nc.vector.tensor_scalar(out=quarter[:], in0=quarter[:], scalar1=0.25, scalar2=None, op0=ALU.add)
+
+        cos_t = keep.tile([P, 32, 2, 2, 4], F32, name="cos_t")
+        sin_t = keep.tile([P, 32, 2, 2, 4], F32, name="sin_t")
+        cos_n = keep.tile([P, 32, 4, 2, 2], F32, name="cos_n")
+        sin_n = keep.tile([P, 32, 4, 2, 2], F32, name="sin_n")
+
+        def table(a, natural):
+            src = (quarter, frac)[a][:].rearrange("p (a u m) -> p a u m", u=2, m=4)
+            for e in range(2):
+                sign = 2 * e - 1 if a else 1
+                if natural:
+                    dst = (cos_n, sin_n)[a][:, :, :, :, e].rearrange("p a m u -> p a u m")
+                else:
+                    dst = (cos_t, sin_t)[a][:, :, :, e, :]
+                nc.scalar.activation(out=dst, in_=src, func=ACT.Sin, scale=sign * 2 * math.pi)
+
+        lw = keep.tile([P, D], F32, name="lw")
+        state = {}
+
+        def lw_turn():
+            for h in range(2):
+                bank = turn_bank("lw_bank%d" % h)
+                for b in range(R):
+                    nc.tensor.transpose(bank[:, b * P:(b + 1) * P], lw_f32[:, h, b:b + 1].to_broadcast([P, P]), ident[:])
+                state["lw", h] = bank
+
+        def lw_copy(h):
+            nc.scalar.copy(out=lw[:, h * N:(h + 1) * N].rearrange("p (q b) -> p q b", b=R), in_=state["lw", h][:].rearrange("p (b q) -> p q b", b=R))
+
+        def copy_on(engine, out, in_):
+            if engine == "V":
+                nc.vector.tensor_copy(out=out, in_=in_)
+            else:
+                nc.scalar.copy(out=out, in_=in_)
+
+        def interleave(engine, key, rows):
+            tile = staged("il_%s%d" % key)
+            copy_on(engine, tile[:].rearrange("p (c i j) -> p c j i", i=4, j=R), rows.rearrange("p j (c i) -> p c j i", i=4))
+            state[key] = tile
+
+        def quantize(key, fmt):
+            codes, scales = operand("%s%d" % key, N)
+            nc.vector.quantize_mx(out=codes[:].bitcast(fmt), scales=scales[:], in_=state[key][:])
+            state["q", key] = (codes, scales)
+
+        def xn_rows(h):
+            tile = ring.tile([P, R, N], BF16, name="xn%d" % h, tag="prod", bufs=2)
+            for j in range(R):
+                nc.vector.scalar_tensor_tensor(out=tile[:, j, :], in0=x_sb[:, j, h * N:(h + 1) * N], scalar=iv[:, j:j + 1], in1=lw[:, h * N:(h + 1) * N], op0=ALU.mult, op1=ALU.mult)
+            state["xn_rows", h] = tile
+
+        def product(k, a):
+            g, jp = divmod(k, 2)
+            if a == 1:
+                state["prod", k] = ring.tile([P, 2, R, 2, P], F32, name="prod%d" % k, tag="prod", bufs=2)
+            table = (cos_t, sin_t)[a]
+            factor = table[:, 16 * jp:16 * jp + 16].rearrange("p (j m) u e i -> p j m (u e) i", j=2).unsqueeze(2).to_broadcast([P, 2, 4, 8, 4, 4])
+            nc.vector.tensor_tensor(
+                out=state["prod", k][:, a].rearrange("p t j (h m i) -> p j h m t i", h=4, i=4),
+                in0=g_sb[g][:, 2 * jp:2 * jp + 2, :].rearrange("p j (h m i t) -> p j h m t i", h=4, i=4, t=4),
+                in1=factor, op=ALU.mult)
+
+        def product_n(k, a):
+            g, jp = divmod(k, 2)
+            if a == 1:
+                state["prod", k] = ring.tile([P, 2, 2, N], F32, name="prod%d" % k, tag="prod", bufs=2)
+            factor = (cos_n, sin_n)[a][:, 16 * jp:16 * jp + 16].rearrange("p (j a) m u e -> p j (a m u e)", j=2).unsqueeze(2).to_broadcast([P, 2, 4, HD])
+            nc.vector.tensor_tensor(
+                out=state["prod", k][:, a].rearrange("p j (h f) -> p j h f", h=4),
+                in0=g_sb[g][:, 2 * jp:2 * jp + 2, :].rearrange("p j (h f) -> p j h f", h=4), in1=factor, op=ALU.mult)
+
+        def rotate_add(k):
+            g, jp = divmod(k, 2)
+            if jp == 0:
+                state["d", g] = ring.tile([P, N * R], BF16, name="d%d" % g, tag="rotated", bufs=2)
+            rows = state["d", g][:].rearrange("p (u j m e) -> p u j m e", u=2, j=R, e=2)
+            prod = state["prod", k]
+            nc.vector.tensor_tensor(
+                out=rows[:, :, 2 * jp:2 * jp + 2].rearrange("p u j m e -> p (j m) u e"),
+                in0=prod[:, 0].rearrange("p j (m u e) -> p (j m) u e", u=2, e=2),
+                in1=prod[:, 1].rearrange("p j (m u e) -> p (j m) u e", u=2, e=2)[:, :, :, ::-1], op=ALU.add)
+
+        def added_turn(k):
+            g, jp = divmod(k, 2)
+            words = state["d", g][:].bitcast(F32).rearrange("p (u j m) -> p u j m", u=2, j=R)
+            bank = turn_bank("added%d" % k)
+            for jj in range(2):
+                for u in range(2):
+                    nc.tensor.transpose(bank[:, (2 * jj + u) * P:(2 * jj + u + 1) * P], words[:, u, 2 * jp + jj, :], ident[:])
+            state["turn", ("f", g), jp] = bank
+
+        def added_interleave(g, engine):
+            tile = staged("il_t%d" % g)
+            copy_on(engine, tile[:].rearrange("p (u c i j) -> p u c j i", u=2, i=4, j=R), state["d", g][:].rearrange("p (u j c i) -> p u c j i", u=2, j=R, i=4))
+            state["t", g] = tile
+
+        def rotate_turn(k, jj):
+            prod = state["prod", k]
+            bank = turn_bank("rot%d_%d" % (k, jj))
+            for t in range(R):
+                nc.tensor.matmul(bank[:, t * P:(t + 1) * P], lhsT=prod[:, 0, t, jj, :], rhs=ident[:], start=True, stop=False, is_transpose=True)
+                nc.tensor.matmul(bank[:, t * P:(t + 1) * P], lhsT=prod[:, 1, t ^ 1, jj, :], rhs=ident[:], start=False, stop=True, is_transpose=True)
+            state["rot", k, jj] = bank
+
+        def rotate_copy(k, jj, engine="S"):
+            g, jp = divmod(k, 2)
+            j = 2 * jp + jj
+            if j == 0:
+                state["f", g] = staged("f%d" % g)
+            copy_on(engine, state["f", g][:, j * N:(j + 1) * N].rearrange("m (p t) -> m p t", t=R), state["rot", k, jj][:].rearrange("m (t p) -> m p t", t=R))
+
+        def back_turn(g):
+            words = state["f", g][:].bitcast(F32).rearrange("m (j p u) -> m j p u", j=R, u=2)
+            for u in range(2):
+                bank = turn_bank("back%d_%d" % (g, u))
+                for j in range(R):
+                    nc.tensor.transpose(bank[:, j * P:(j + 1) * P], words[:, j, :, u], ident[:])
+                state["back", g, u] = bank
+
+        def back_copy(g, u, engine="S"):
+            if u == 0:
+                state["t", g] = staged("t%d" % g)
+            copy_on(engine, state["t", g][:, u * 2 * N:(u + 1) * 2 * N].rearrange("p (c j) -> p c j", j=R), state["back", g, u][:].bitcast(BF16).rearrange("p (j c) -> p c j", j=R))
+
+        def word_turn(key):
+            if key[0] == "f":
+                words = g_sb[key[1]][:].rearrange("p r c -> p (r c)").bitcast(F32).rearrange("p (r w) -> p r w", r=R)
+            else:
+                h, g = divmod(key[1], 6)
+                words = w_sb[g // 2, h][:].rearrange("p r c -> p (r c)").bitcast(F32).rearrange("p (r w) -> p r w", r=R)[:, :, (g % 2) * 256:(g % 2 + 1) * 256]
+            for half in range(2):
+                bank = turn_bank("turn_%s%d_%d" % (key + (half,)))
+                for rr in range(2):
+                    for u in range(2):
+                        nc.tensor.transpose(bank[:, (2 * rr + u) * P:(2 * rr + u + 1) * P], words[:, 2 * half + rr, u:256:2], ident[:])
+                state["turn", key, half] = bank
+
+        def word_copy(key, half, engine="S"):
+            if half == 0:
+                state[key] = staged("st_%s%d" % key)
+            words = state[key][:].bitcast(F32)[:, half * N:(half + 1) * N]
+            copy_on(engine, words.rearrange("m (r p u) -> m r p u", r=2, u=2), state["turn", key, half][:].rearrange("m (r u p) -> m r p u", r=2, u=2))
+
+        def dw_mm(i, b, halves=(0, 1)):
+            xc, xs = state["q", ("xn", b // 4)]
+            cols = slice((b % 4) * P, (b % 4 + 1) * P)
+            for gg in halves:
+                zc, zs = state["q", ("t", 2 * i + gg)]
+                bank = (turn_bank if state.get("late") else sum_bank)("dw%d_%d_%d" % (i, b, gg))
+                nc.tensor.matmul_mx(out=bank[:], lhsT=xc[:, cols].bitcast(E4), lhsT_scale=xs[:, cols], rhs=zc[:].bitcast(E5), rhs_scale=zs[:], start=True, stop=True)
+                state["dw", i, b, gg] = bank
+
+        def dw_copy(i, b, gg, engine="S"):
+            key = ("dw_rows", i, b)
+            if key not in state:
+                state[key] = ring.tile([P, J], F32, name="dw_rows%d_%d" % (i, b), tag="rows", bufs=6)
+            dst = state[key][:, gg * N:(gg + 1) * N]
+            bank = state["dw", i, b, gg]
+            if i < 2:
+                copy_on(engine, dst.rearrange("p (m u e) -> p m u e", u=2, e=2), bank[:].rearrange("p (u m e) -> p m u e", u=2, e=2))
+            else:
+                copy_on(engine, dst, bank[:])
+
+        def dw_store(i, b):
+            nc.sync.dma_start(out=dw_out[i][b * P:(b + 1) * P, :], in_=state["dw_rows", i, b][:])
+
+        def dx_mm(h, j, passes):
+            if ("dx", h, j) not in state:
+                state["dx", h, j] = sum_bank("dx%d_%d" % (h, j))
+            cols = slice(j * P, (j + 1) * P)
+            for g in passes:
+                zc, zs = state["q", ("f", g)]
+                wc, ws = state["q", ("w", 6 * h + g)]
+                nc.tensor.matmul_mx(out=state["dx", h, j][:], lhsT=zc[:, cols].bitcast(E5), lhsT_scale=zs[:, cols], rhs=wc[:].bitcast(E4), rhs_scale=ws[:], start=(g == ORDER[0]), stop=(g == ORDER[-1]))
+
+        part = keep.tile([P, R, 2], F32, name="part")
+        coef = keep.tile([P, R], F32, name="coef")
+
+        def gain(h, j):
+            if h == 0 and j % 2 == 0:
+                state["g", j // 2] = ring.tile([P, 2, D], F32, name="gain%d" % j, tag="prod", bufs=2)
+            cols = slice(h * N, (h + 1) * N)
+            nc.vector.scalar_tensor_tensor(
+                out=state["g", j // 2][:, j % 2, cols].rearrange("p (q b) -> p q b", b=R),
+                in0=state["dx", h, j][:].rearrange("p (b q) -> p q b", b=R), scalar=iv[:, j:j + 1],
+                in1=lw[:, cols].rearrange("p (q b) -> p q b", b=R), op0=ALU.mult, op1=ALU.mult)
+
+        def row_sum(h, j):
+            cols = slice(h * N, (h + 1) * N)
+            terms = ring.tile([P, N], F32, name="terms%d_%d" % (h, j), tag="rotated", bufs=2)
+            nc.vector.scalar_tensor_tensor(out=terms[:], in0=state["g", j // 2][:, j % 2, cols], scalar=mean_coef[:, j:j + 1], in1=x_sb[:, j, cols], op0=ALU.mult, op1=ALU.mult, accum_out=part[:, j, h:h + 1])
+
+        def join_sum(j):
+            nc.vector.tensor_tensor(out=coef[:, j:j + 1], in0=part[:, j, 0:1], in1=part[:, j, 1:2], op=ALU.add)
+
+        def finish(j):
+            rows = state["g", j // 2][:, j % 2, :]
+            nc.vector.scalar_tensor_tensor(out=rows, in0=x_sb[:, j, :], scalar=coef[:, j:j + 1], in1=rows, op0=ALU.mult, op1=ALU.add)
+            nc.sync.dma_start(out=out_0.rearrange("b (p j) d -> p (b j) d", j=R)[:, j, :], in_=rows)
+
+        def dw(i, b, engines="SS"):
+            dw_mm(i, b)
+            dw_copy(i, b, 0, engines[0])
+            dw_copy(i, b, 1, engines[1])
+            dw_store(i, b)
+
+        def wturn(n, engines="SS"):
+            word_turn(("w", n))
+            word_copy(("w", n), 0, engines[0])
+            word_copy(("w", n), 1, engines[1])
+
+        def rot(k):
+            rotate_turn(k, 0)
+            rotate_turn(k, 1)
+            rotate_copy(k, 0)
+            rotate_copy(k, 1)
+
+        def back(g):
+            back_turn(g)
+            back_copy(g, 0)
+            back_copy(g, 1)
+
+        def added(k):
+            added_turn(k)
+            word_copy(("f", k // 2), k % 2)
+
+        def prod(k):
+            product(k, 1)
+            product(k, 0)
+
+        def prod_n(k):
+            product_n(k, 1)
+            product_n(k, 0)
+
+        def half_dw(i, b, gg):
+            dw_mm(i, b, (gg,))
+            dw_copy(i, b, gg)
+            if gg:
+                dw_store(i, b)
+
+        def q(kind, n):
+            quantize((kind, n), E5 if kind in "tf" else E4)
+
+        dws = [(2, b) for b in range(4, 8)] + [(0, b) for b in range(8)] + [(1, b) for b in range(8)]
+        def d(engines="SS"):
+            dw(*dws.pop(0), engines)
+
+        table(1, False)
+        lw_turn()
+        interleave("V", ("t", 4), g_sb[4][:])
+        lw_copy(0)
+        table(0, False)
+        lw_copy(1)
+        word_turn(("f", 4))
+        xn_rows(0)
+        word_copy(("f", 4), 0)
+        word_copy(("f", 4), 1)
+        table(1, True)
+        table(0, True)
+        q("t", 4)
+        interleave("S", ("xn", 0), state["xn_rows", 0][:])
+        prod(0)
+        word_turn(("f", 5))
+        q("xn", 0)
+        interleave("V", ("t", 5), g_sb[5][:])
+        word_copy(("f", 5), 0)
+        word_copy(("f", 5), 1)
+        half_dw(2, 0, 0)
+        half_dw(2, 1, 0)
+        rot(0)
+        product(1, 1)
+        q("t", 5)
+        product(1, 0)
+        half_dw(2, 2, 0)
+        half_dw(2, 3, 0)
+        wturn(0)
+        q("f", 4)
+        xn_rows(1)
+        half_dw(2, 0, 1)
+        rot(1)
+        half_dw(2, 1, 1)
+        half_dw(2, 2, 1)
+        q("f", 5)
+        interleave("V", ("xn", 1), state["xn_rows", 1][:])
+        q("w", 0)
+        q("f", 0)
+        wturn(1)
+        half_dw(2, 3, 1)
+        product(2, 1)
+        q("xn", 1)
+        product(2, 0)
+        wturn(4)
+        back(0)
+        q("w", 1)
+        prod(3)
+        d()
+        rot(2)
+        q("w", 4)
+        q("t", 0)
+        wturn(5)
+        d()
+        prod_n(4)
+        rot(3)
+        q("w", 5)
+        rotate_add(4)
+        d()
+        q("f", 1)
+        wturn(2)
+        prod_n(5)
+        d()
+        back(1)
+        state["late"] = True
+        q("w", 2)
+        rotate_add(5)
+        dx_mm(0, 0, (0, 1, 4, 5))
+        added(4)
+        wturn(3)
+        q("t", 1)
+        added_interleave(2, "V")
+        dx_mm(0, 1, (0, 1, 4, 5))
+        added(5)
+        prod_n(6)
+        d()
+        wturn(6)
+        dx_mm(0, 2, (0, 1, 4, 5))
+        q("w", 3)
+        q("f", 2)
+        rotate_add(6)
+        d()
+        q("t", 2)
+        dx_mm(0, 3, (0, 1, 4, 5))
+        d()
+        prod_n(7)
+        wturn(7)
+        added(6)
+        q("w", 6)
+        rotate_add(7)
+        d()
+        for j in range(4):
+            dx_mm(0, j, (2,))
+        d()
+        q("w", 7)
+        added_interleave(3, "V")
+        added(7)
+        wturn(8)
+        d()
+        q("f", 3)
+        q("t", 3)
+        wturn(9)
+        q("w", 8)
+        for j in range(4):
+            dx_mm(0, j, (3,))
+        d()
+        gain(0, 0)
+        gain(0, 1)
+        wturn(10)
+        q("w", 9)
+        gain(0, 2)
+        gain(0, 3)
+        d()
+        dx_mm(1, 0, (0, 1))
+        wturn(11)
+        row_sum(0, 0)
+        q("w", 10)
+        row_sum(0, 1)
+        dx_mm(1, 1, (0, 1))
+        d()
+        dx_mm(1, 2, (0, 1))
+        row_sum(0, 2)
+        q("w", 11)
+        row_sum(0, 3)
+        d()
+        dx_mm(1, 0, (4, 5, 2, 3))
+        d()
+        dx_mm(1, 1, (4, 5, 2, 3))
+        gain(1, 0)
+        d()
+        dx_mm(1, 2, (4, 5, 2, 3))
+        row_sum(1, 0)
+        gain(1, 1)
+        join_sum(0)
+        d()
+        row_sum(1, 1)
+        finish(0)
+        dx_mm(1, 3, ORDER)
+        join_sum(1)
+        gain(1, 2)
+        d()
+        finish(1)
+        row_sum(1, 2)
+        d()
+        gain(1, 3)
+        join_sum(2)
+        row_sum(1, 3)
+        d()
+        finish(2)
+        join_sum(3)
+        finish(3)
+        assert not dws

@@ -77,12 +77,13 @@ def tile_pagedllamablock_pa_v_kernel(tc, x, ln_w, wq, wk, wv, inv_rms, grad_0, g
         load_g(1)
         load_x(1)
         load_w(0, 0)
-        load_w(2, 0)
         load_g(2)
-        load_w(1, 0)
+        load_w(0, 1)
         load_g(3)
-        for i in range(3):
-            load_w(i, 1)
+        load_w(2, 0)
+        load_w(2, 1)
+        load_w(1, 0)
+        load_w(1, 1)
 
         pos = keep.tile([P, R], I32, name="pos")
         nc.gpsimd.iota(pos[:], pattern=[[1, R]], base=0, channel_multiplier=R)
@@ -108,8 +109,7 @@ def tile_pagedllamablock_pa_v_kernel(tc, x, ln_w, wq, wk, wv, inv_rms, grad_0, g
         nc.vector.scalar_tensor_tensor(out=quarter[:], in0=frac[:], scalar=-1.0, in1=frac[:], op0=ALU.mult, op1=ALU.min)
         nc.vector.tensor_scalar(out=quarter[:], in0=quarter[:], scalar1=0.25, scalar2=None, op0=ALU.add)
 
-        cos_t = keep.tile([P, 32, 2, 2, 4], F32, name="cos_t")
-        sin_t = keep.tile([P, 32, 2, 2, 4], F32, name="sin_t")
+        cos_t = sin_t = None
         cos_n = keep.tile([P, 32, 4, 2, 2], F32, name="cos_n")
         sin_n = keep.tile([P, 32, 4, 2, 2], F32, name="sin_n")
 
@@ -262,7 +262,7 @@ def tile_pagedllamablock_pa_v_kernel(tc, x, ln_w, wq, wk, wv, inv_rms, grad_0, g
         def dw_copy(i, b, gg, engine="S"):
             key = ("dw_rows", i, b)
             if key not in state:
-                state[key] = ring.tile([P, J], F32, name="dw_rows%d_%d" % (i, b), tag="rows", bufs=6)
+                state[key] = ring.tile([P, J], F32, name="dw_rows%d_%d" % (i, b), tag="rows", bufs=7)
             dst = state[key][:, gg * N:(gg + 1) * N]
             bank = state["dw", i, b, gg]
             if i < 2:
@@ -350,159 +350,104 @@ def tile_pagedllamablock_pa_v_kernel(tc, x, ln_w, wq, wk, wv, inv_rms, grad_0, g
         def q(kind, n):
             quantize((kind, n), E5 if kind in "tf" else E4)
 
-        dws = [(2, b) for b in range(4, 8)] + [(0, b) for b in range(8)] + [(1, b) for b in range(8)]
+        dws = [(2, b) for b in range(0, 8)] + [(0, b) for b in range(8)] + [(1, b) for b in range(8)]
         def d(engines="SS"):
             dw(*dws.pop(0), engines)
 
-        table(1, False)
+        state["late"] = True
+        table(1, True)
         lw_turn()
         interleave("V", ("t", 4), g_sb[4][:])
         lw_copy(0)
-        table(0, False)
+        table(0, True)
         lw_copy(1)
         word_turn(("f", 4))
         xn_rows(0)
         word_copy(("f", 4), 0)
         word_copy(("f", 4), 1)
-        table(1, True)
-        table(0, True)
         q("t", 4)
         interleave("S", ("xn", 0), state["xn_rows", 0][:])
-        prod(0)
         word_turn(("f", 5))
-        q("xn", 0)
-        interleave("V", ("t", 5), g_sb[5][:])
         word_copy(("f", 5), 0)
         word_copy(("f", 5), 1)
-        half_dw(2, 0, 0)
-        half_dw(2, 1, 0)
-        rot(0)
-        product(1, 1)
-        q("t", 5)
-        product(1, 0)
-        half_dw(2, 2, 0)
-        half_dw(2, 3, 0)
-        wturn(0)
-        q("f", 4)
-        xn_rows(1)
-        half_dw(2, 0, 1)
-        rot(1)
-        half_dw(2, 1, 1)
-        half_dw(2, 2, 1)
-        q("f", 5)
-        interleave("V", ("xn", 1), state["xn_rows", 1][:])
-        q("w", 0)
-        q("f", 0)
-        wturn(1)
-        half_dw(2, 3, 1)
-        product(2, 1)
-        q("xn", 1)
-        product(2, 0)
-        wturn(4)
-        back(0)
-        q("w", 1)
-        prod(3)
-        d()
-        rot(2)
-        q("w", 4)
-        q("t", 0)
-        wturn(5)
-        d()
-        prod_n(4)
-        rot(3)
-        q("w", 5)
-        rotate_add(4)
-        d()
-        q("f", 1)
-        wturn(2)
-        prod_n(5)
-        d()
-        back(1)
-        state["late"] = True
-        q("w", 2)
-        rotate_add(5)
-        dx_mm(0, 0, (0, 1, 4, 5))
-        added(4)
-        wturn(3)
-        q("t", 1)
-        added_interleave(2, "V")
-        dx_mm(0, 1, (0, 1, 4, 5))
-        added(5)
-        prod_n(6)
-        d()
-        wturn(6)
-        dx_mm(0, 2, (0, 1, 4, 5))
-        q("w", 3)
-        q("f", 2)
-        rotate_add(6)
-        d()
-        q("t", 2)
-        dx_mm(0, 3, (0, 1, 4, 5))
-        d()
-        prod_n(7)
-        wturn(7)
-        added(6)
-        q("w", 6)
-        rotate_add(7)
-        d()
-        for j in range(4):
-            dx_mm(0, j, (2,))
-        d()
-        q("w", 7)
-        added_interleave(3, "V")
+        interleave("S", ("t", 5), g_sb[5][:])
+        units = [6 * h + g for g in ORDER for h in range(2)]
+        ready = [("xn", 0)]
+        soon = [("f", 4), ("t", 5)]
+        nd = [0,0, 0,1, 1,1, 1,2, 1,1, 1,1, 1,1, 2,0]
+        nw = [0,0, 1,1, 1,1, 1,1, 1,1, 1,1, 1,1, 0,0]
+        il = "VVVV"
+        passes = [(),(),(),(0,),(),(1,4),(5,),(2,),(3,)]
+
+        def side_work(nunits, njobs, engines="SS"):
+            for n in range(max(nunits, njobs)):
+                if n < nunits:
+                    unit = units.pop(0)
+                    wturn(unit)
+                    soon.append(("w", unit))
+                if n < njobs:
+                    d()
+
+        def flush():
+            for key in ready:
+                q(*key)
+            ready.clear()
+            ready.extend(soon)
+            soon.clear()
+
+        for k in range(8):
+            prod_n(k)
+            if k == 99:
+                state["late"] = True
+            if k:
+                added(k - 1)
+                if k % 2 == 0:
+                    soon.append(("f", k // 2 - 1))
+                    if il[k // 2 - 1] == "S":
+                        added_interleave(k // 2 - 1, "S")
+                        soon.append(("t", k // 2 - 1))
+            side_work(nw[2 * k], nd[2 * k])
+            flush()
+            rotate_add(k)
+            if k == 0:
+                xn_rows(1)
+                interleave("S", ("xn", 1), state["xn_rows", 1][:])
+                soon.extend([("xn", 1), ("f", 5)])
+            for g in passes[k]:
+                for j in range(2):
+                    for h in range(2):
+                        dx_mm(h, j, (g,))
+            side_work(nw[2 * k + 1], nd[2 * k + 1])
+            flush()
+            if k % 2 == 1 and il[k // 2] == "V":
+                added_interleave(k // 2, "V")
+                ready.append(("t", k // 2))
         added(7)
-        wturn(8)
-        d()
+        side_work(0, 2)
         q("f", 3)
-        q("t", 3)
-        wturn(9)
-        q("w", 8)
+        flush()
+        flush()
+        for j in range(2):
+            for h in range(2):
+                dx_mm(h, j, passes[8])
+        tail = ["xd","xddxd","xdd",""]
+        later = [(h, j) for j in (2, 3) for h in range(2)]
+        d()
+        d()
         for j in range(4):
-            dx_mm(0, j, (3,))
-        d()
-        gain(0, 0)
-        gain(0, 1)
-        wturn(10)
-        q("w", 9)
-        gain(0, 2)
-        gain(0, 3)
-        d()
-        dx_mm(1, 0, (0, 1))
-        wturn(11)
-        row_sum(0, 0)
-        q("w", 10)
-        row_sum(0, 1)
-        dx_mm(1, 1, (0, 1))
-        d()
-        dx_mm(1, 2, (0, 1))
-        row_sum(0, 2)
-        q("w", 11)
-        row_sum(0, 3)
-        d()
-        dx_mm(1, 0, (4, 5, 2, 3))
-        d()
-        dx_mm(1, 1, (4, 5, 2, 3))
-        gain(1, 0)
-        d()
-        dx_mm(1, 2, (4, 5, 2, 3))
-        row_sum(1, 0)
-        gain(1, 1)
-        join_sum(0)
-        d()
-        row_sum(1, 1)
-        finish(0)
-        dx_mm(1, 3, ORDER)
-        join_sum(1)
-        gain(1, 2)
-        d()
-        finish(1)
-        row_sum(1, 2)
-        d()
-        gain(1, 3)
-        join_sum(2)
-        row_sum(1, 3)
-        d()
-        finish(2)
+            gain(0, j)
+            if j:
+                join_sum(j - 1)
+            gain(1, j)
+            if j:
+                finish(j - 1)
+            for c in tail[j]:
+                if c == "d":
+                    d()
+                else:
+                    dx_mm(*later.pop(0), ORDER)
+            row_sum(0, j)
+            row_sum(1, j)
         join_sum(3)
         finish(3)
         assert not dws

@@ -22,10 +22,25 @@ ACT = mybir.ActivationFunctionType
 P = 128
 R = 4
 N = 512
-ORDER = (0, 1, 4, 5, 2, 3)
+CHUNK = R * N
+PAIRS = R * HD // 2
+BANKS = 8
+Q_K_CHUNKS = (0, 1, 2, 3)
+V_CHUNKS = (4, 5)
+PASS_ORDER = V_CHUNKS + Q_K_CHUNKS
+COS, SIN = 0, 1
+
+GPSIMD_COLUMNS = 1664
+JOBS_BESIDE, JOBS_AFTER = 4, 4
+LAST_JOBS_BESIDE, LAST_JOBS_AFTER = 3, 2
+ROW_TILES = 7
+WIDE_TILES = 4
+STAGING_TILES = 3
 
 
-def tile_pagedllamablock_pa_v_kernel(tc, x, ln_w, wq, wk, wv, inv_rms, grad_0, grad_1, grad_2, out_0, out_1, out_2, out_3):
+def tile_pagedllamablock_pa_v_kernel(
+    tc, x, ln_w, wq, wk, wv, inv_rms, grad_0, grad_1, grad_2, out_0, out_1, out_2, out_3
+):
     nc = tc.nc
     weights = (wq, wk, wv)
     grads = (grad_0, grad_1, grad_2)
@@ -37,417 +52,370 @@ def tile_pagedllamablock_pa_v_kernel(tc, x, ln_w, wq, wk, wv, inv_rms, grad_0, g
         psum = ctx.enter_context(tc.psum_pool(name="psum", bufs=1))
         ctx.enter_context(tc.manual_schedule())
 
-        def turn_bank(name):
-            return psum.tile([P, N], F32, name=name, tag="turn", bufs=4)
+        rotation = list(range(BANKS))
+        held = {}
 
-        def sum_bank(name):
-            return psum.tile([P, N], F32, name=name, tag="sum", bufs=4)
+        def next_bank(name):
+            number = rotation.pop(0)
+            rotation.append(number)
+            return psum.tile([P, N], F32, name=name, tag="bank%d" % number)
 
-        def staged(name):
-            return ring.tile([P, N * R], BF16, name=name, tag="staged", bufs=7, align_bytes=64)
+        def hold_bank(name):
+            held[name] = rotation.pop(0)
+            return psum.tile([P, N], F32, name=name, tag="bank%d" % held[name])
 
-        def operand(name, width):
-            codes = keep.tile([P, width], U32, name=name + "_codes", align_bytes=64)
-            scales = keep.tile([P, width], U8, name=name + "_scales", align_bytes=64)
-            return codes, scales
+        def release_bank(name):
+            rotation.append(held[name])
 
-        iv = keep.tile([P, R], F32, name="iv")
+        def row_tile(name):
+            return ring.tile([P, J], F32, name=name, tag="rows", bufs=ROW_TILES, align_bytes=64)
+
+        def wide_tile(name):
+            return ring.tile([P, CHUNK], F32, name=name, tag="wide", bufs=WIDE_TILES)
+
+        def staging_tile(name):
+            return ring.tile([P, 2 * CHUNK], BF16, name=name, tag="staging", bufs=STAGING_TILES, align_bytes=64)
+
+        def gpsimd_tile(name, shape, dtype):
+            return ring.tile(shape, dtype, name=name, tag="gpsimd", bufs=1, align_bytes=64)
+
+        def by_row(ap):
+            return ap.rearrange("p (r c) -> p r c", r=R)
+
+        def half(h):
+            return slice(h * N, (h + 1) * N)
+
+        def block(b):
+            return slice(b * P, (b + 1) * P)
+
+        inv = keep.tile([P, R], F32, name="inv")
         lw_cols = keep.tile([P, 2, R], BF16, name="lw_cols")
         x_sb = keep.tile([P, R, D], BF16, name="x_sb")
-        g_sb = [keep.tile([P, R, N], BF16, name="g%d" % g) for g in range(6)]
-        w_sb = {(i, h): keep.tile([P, R, J], BF16, name="w%d%d" % (i, h)) for i in range(3) for h in range(2)}
+        v_rows = wide_tile("v_rows")[:].bitcast(BF16)
+        grad_sb = [keep.tile([P, CHUNK], BF16, name="grad%d" % g)[:] for g in Q_K_CHUNKS]
+        grad_sb.extend([v_rows[:, :CHUNK], v_rows[:, CHUNK:]])
+        w_sb = {(i, h): keep.tile([P, R * J], BF16, name="w%d%d" % (i, h)) for i in range(3) for h in range(2)}
 
-        def load_g(g):
+        def load_grad(g):
             rows = grads[g // 2].rearrange("b (p j) h e -> p (b j) (h e)", j=R)
-            nc.sync.dma_start(out=g_sb[g][:], in_=rows[:, :, (g % 2) * N:(g % 2 + 1) * N])
+            nc.sync.dma_start(out=by_row(grad_sb[g]), in_=rows[:, :, half(g % 2)])
 
         def load_x(h):
             rows = x.rearrange("b (p j) d -> p (b j) d", j=R)
-            nc.sync.dma_start(out=x_sb[:, :, h * N:(h + 1) * N], in_=rows[:, :, h * N:(h + 1) * N])
+            nc.sync.dma_start(out=x_sb[:, :, half(h)], in_=rows[:, :, half(h)])
 
         def load_w(i, h):
-            nc.sync.dma_start(out=w_sb[i, h][:], in_=weights[i][h * N:(h + 1) * N, :].rearrange("(p b) c -> p b c", b=R))
+            nc.sync.dma_start(out=w_sb[i, h][:], in_=weights[i][half(h), :].rearrange("(p b) c -> p (b c)", b=R))
 
         nc.sync.dma_start(out=lw_cols[:], in_=ln_w.rearrange("(h p b) -> p h b", h=2, b=R))
-        nc.sync.dma_start(out=iv[:], in_=inv_rms.rearrange("b (p j) o -> p (b j o)", j=R))
-        load_g(4)
+        nc.sync.dma_start(out=inv[:], in_=inv_rms.rearrange("b (p j) o -> p (b j o)", j=R))
         load_x(0)
-        load_g(0)
-        load_g(5)
-        load_g(1)
+        load_grad(4)
         load_x(1)
-        load_w(0, 0)
-        load_g(2)
-        load_w(0, 1)
-        load_g(3)
         load_w(2, 0)
+        load_grad(5)
+        load_grad(0)
         load_w(2, 1)
+        load_grad(1)
+        load_w(0, 0)
+        load_w(0, 1)
+        load_grad(2)
         load_w(1, 0)
         load_w(1, 1)
+        load_grad(3)
 
-        pos = keep.tile([P, R], I32, name="pos")
-        nc.gpsimd.iota(pos[:], pattern=[[1, R]], base=0, channel_multiplier=R)
+        position = keep.tile([P, R], I32, name="position")
+        nc.gpsimd.iota(position[:], pattern=[[1, R]], base=0, channel_multiplier=R)
         ident = keep.tile([P, P], F32, name="ident")
         make_identity(nc, ident[:])
 
-        turns = keep.tile([P, R, 8, 8], F32, name="turns")
-        for u in range(2):
-            for mi in range(4):
-                nc.vector.tensor_scalar(out=turns[:, :, 0, 4 * u + mi], in0=pos[:], scalar1=THETA ** (-(2 * mi + u) / 64) / (2 * math.pi), scalar2=None, op0=ALU.mult)
-        for mm in range(1, 8):
-            nc.vector.tensor_scalar(out=turns[:, :, mm, :], in0=turns[:, :, 0, :], scalar1=THETA ** (-mm / 8), scalar2=None, op0=ALU.mult)
-        flat = turns[:].rearrange("p j a b -> p (j a b)")
-        whole = keep.tile([P, 256], I32, name="whole")
-        nc.vector.tensor_copy(out=whole[:], in_=flat)
+        scratch = row_tile("angle_scratch")
+        turns = scratch[:, :PAIRS]
+        whole_turns = scratch[:, PAIRS:2 * PAIRS].bitcast(I32)
+        by_frequency = turns.rearrange("p (j a b) -> p j a b", j=R, a=8)
+        for b in range(8):
+            nc.vector.tensor_scalar(
+                out=by_frequency[:, :, 0, b], in0=position[:], scalar1=THETA ** (-b / 64) / (2 * math.pi),
+                scalar2=None, op0=ALU.mult)
+        for a in range(1, 8):
+            nc.vector.tensor_scalar(
+                out=by_frequency[:, :, a, :], in0=by_frequency[:, :, 0, :], scalar1=THETA ** (-a / 8),
+                scalar2=None, op0=ALU.mult)
         lw_f32 = keep.tile([P, 2, R], F32, name="lw_f32")
         nc.vector.tensor_copy(out=lw_f32[:], in_=lw_cols[:])
-        frac = keep.tile([P, 256], F32, name="frac")
-        nc.vector.tensor_tensor(out=frac[:], in0=flat, in1=whole[:], op=ALU.subtract)
-        mean_coef = keep.tile([P, R], F32, name="mean_coef")
-        nc.vector.scalar_tensor_tensor(out=mean_coef[:], in0=iv[:], scalar=-1.0 / D, in1=iv[:], op0=ALU.mult, op1=ALU.mult)
-        quarter = keep.tile([P, 256], F32, name="quarter")
-        nc.vector.scalar_tensor_tensor(out=quarter[:], in0=frac[:], scalar=-1.0, in1=frac[:], op0=ALU.mult, op1=ALU.min)
-        nc.vector.tensor_scalar(out=quarter[:], in0=quarter[:], scalar1=0.25, scalar2=None, op0=ALU.add)
+        nc.vector.tensor_copy(out=whole_turns, in_=turns)
+        mean_factor = keep.tile([P, R], F32, name="mean_factor")
+        nc.vector.scalar_tensor_tensor(
+            out=mean_factor[:], in0=inv[:], scalar=-1.0 / D, in1=inv[:], op0=ALU.mult, op1=ALU.mult)
+        angles = gpsimd_tile("angles", [P, 2 * N], F32)
+        signed = angles[:, half(SIN)].rearrange("p (i e) -> p i e", e=2)
+        nc.vector.tensor_tensor(out=signed[:, :, 0], in0=turns, in1=whole_turns, op=ALU.subtract)
+        nc.vector.tensor_tensor(out=signed[:, :, 1], in0=whole_turns, in1=turns, op=ALU.subtract)
+        nc.vector.tensor_tensor(
+            out=angles[:, half(COS)].rearrange("p (i e) -> p i e", e=2), in0=signed, in1=signed[:, :, ::-1],
+            op=ALU.min)
 
-        cos_t = sin_t = None
-        cos_n = keep.tile([P, 32, 4, 2, 2], F32, name="cos_n")
-        sin_n = keep.tile([P, 32, 4, 2, 2], F32, name="sin_n")
+        flipped = row_tile("flipped_tables")
+        tables = {}
 
-        def table(a, natural):
-            src = (quarter, frac)[a][:].rearrange("p (a u m) -> p a u m", u=2, m=4)
-            for e in range(2):
-                sign = 2 * e - 1 if a else 1
-                if natural:
-                    dst = (cos_n, sin_n)[a][:, :, :, :, e].rearrange("p a m u -> p a u m")
-                else:
-                    dst = (cos_t, sin_t)[a][:, :, :, e, :]
-                nc.scalar.activation(out=dst, in_=src, func=ACT.Sin, scale=sign * 2 * math.pi)
+        def flip_angles(table):
+            bank = next_bank("flipped_angles%d" % table)
+            for j in range(R):
+                nc.tensor.transpose(bank[:, block(j)], angles[:, half(table)][:, block(j)], ident[:])
+            nc.scalar.activation(
+                out=flipped[:, half(table)], in_=bank[:], func=ACT.Sin, scale=2 * math.pi,
+                bias=math.pi / 2 if table == COS else 0.0)
+
+        def flip_back(table):
+            tables[table] = hold_bank("table%d" % table)
+            for j in range(R):
+                nc.tensor.transpose(tables[table][:, block(j)], flipped[:, half(table)][:, block(j)], ident[:])
 
         lw = keep.tile([P, D], F32, name="lw")
-        state = {}
+        lw_bank = {}
 
-        def lw_turn():
+        def spread_lw(h):
+            lw_bank[h] = hold_bank("lw%d" % h)
+            for b in range(R):
+                nc.tensor.transpose(lw_bank[h][:, b:N:R], lw_f32[:, h, b:b + 1].to_broadcast([P, P]), ident[:])
+            nc.scalar.copy(out=lw[:, half(h)], in_=lw_bank[h][:])
+
+        staged = {}
+        mx = {}
+
+        def quantize(key, first=0, width=None):
+            total = N if key[0] == "xn" else 2 * N
+            width = width or total
+            if key not in mx:
+                name = "_".join(map(str, key))
+                codes = keep.tile([P, total], U32, name=name + "_codes", align_bytes=64)
+                scales = keep.tile([P, total], U8, name=name + "_scales", align_bytes=64)
+                mx[key] = (codes, scales)
+            codes, scales = mx[key]
+            cols = slice(first, first + width)
+            nc.vector.quantize_mx(
+                out=codes[:, cols].bitcast(E5 if key[0] == "dz" else E4), scales=scales[:, cols],
+                in_=staged[key][:, R * first:R * (first + width)])
+
+        def interleave(copy, dst, rows):
+            copy(out=dst.rearrange("p (c i j) -> p c j i", i=4, j=R),
+                 in_=rows.rearrange("p (j c i) -> p c j i", j=R, i=4))
+
+        def turn_words(name, rows, first_word, dst):
+            words = by_row(rows.bitcast(F32))
+            banks = [next_bank("%s_%d" % (name, h)) for h in range(2)]
             for h in range(2):
-                bank = turn_bank("lw_bank%d" % h)
-                for b in range(R):
-                    nc.tensor.transpose(bank[:, b * P:(b + 1) * P], lw_f32[:, h, b:b + 1].to_broadcast([P, P]), ident[:])
-                state["lw", h] = bank
-
-        def lw_copy(h):
-            nc.scalar.copy(out=lw[:, h * N:(h + 1) * N].rearrange("p (q b) -> p q b", b=R), in_=state["lw", h][:].rearrange("p (b q) -> p q b", b=R))
-
-        def copy_on(engine, out, in_):
-            if engine == "V":
-                nc.vector.tensor_copy(out=out, in_=in_)
-            else:
-                nc.scalar.copy(out=out, in_=in_)
-
-        def interleave(engine, key, rows):
-            tile = staged("il_%s%d" % key)
-            copy_on(engine, tile[:].rearrange("p (c i j) -> p c j i", i=4, j=R), rows.rearrange("p j (c i) -> p c j i", i=4))
-            state[key] = tile
-
-        def quantize(key, fmt):
-            codes, scales = operand("%s%d" % key, N)
-            nc.vector.quantize_mx(out=codes[:].bitcast(fmt), scales=scales[:], in_=state[key][:])
-            state["q", key] = (codes, scales)
-
-        def xn_rows(h):
-            tile = ring.tile([P, R, N], BF16, name="xn%d" % h, tag="prod", bufs=2)
-            for j in range(R):
-                nc.vector.scalar_tensor_tensor(out=tile[:, j, :], in0=x_sb[:, j, h * N:(h + 1) * N], scalar=iv[:, j:j + 1], in1=lw[:, h * N:(h + 1) * N], op0=ALU.mult, op1=ALU.mult)
-            state["xn_rows", h] = tile
-
-        def product(k, a):
-            g, jp = divmod(k, 2)
-            if a == 1:
-                state["prod", k] = ring.tile([P, 2, R, 2, P], F32, name="prod%d" % k, tag="prod", bufs=2)
-            table = (cos_t, sin_t)[a]
-            factor = table[:, 16 * jp:16 * jp + 16].rearrange("p (j m) u e i -> p j m (u e) i", j=2).unsqueeze(2).to_broadcast([P, 2, 4, 8, 4, 4])
-            nc.vector.tensor_tensor(
-                out=state["prod", k][:, a].rearrange("p t j (h m i) -> p j h m t i", h=4, i=4),
-                in0=g_sb[g][:, 2 * jp:2 * jp + 2, :].rearrange("p j (h m i t) -> p j h m t i", h=4, i=4, t=4),
-                in1=factor, op=ALU.mult)
-
-        def product_n(k, a):
-            g, jp = divmod(k, 2)
-            if a == 1:
-                state["prod", k] = ring.tile([P, 2, 2, N], F32, name="prod%d" % k, tag="prod", bufs=2)
-            factor = (cos_n, sin_n)[a][:, 16 * jp:16 * jp + 16].rearrange("p (j a) m u e -> p j (a m u e)", j=2).unsqueeze(2).to_broadcast([P, 2, 4, HD])
-            nc.vector.tensor_tensor(
-                out=state["prod", k][:, a].rearrange("p j (h f) -> p j h f", h=4),
-                in0=g_sb[g][:, 2 * jp:2 * jp + 2, :].rearrange("p j (h f) -> p j h f", h=4), in1=factor, op=ALU.mult)
-
-        def rotate_add(k):
-            g, jp = divmod(k, 2)
-            if jp == 0:
-                state["d", g] = ring.tile([P, N * R], BF16, name="d%d" % g, tag="rotated", bufs=2)
-            rows = state["d", g][:].rearrange("p (u j m e) -> p u j m e", u=2, j=R, e=2)
-            prod = state["prod", k]
-            nc.vector.tensor_tensor(
-                out=rows[:, :, 2 * jp:2 * jp + 2].rearrange("p u j m e -> p (j m) u e"),
-                in0=prod[:, 0].rearrange("p j (m u e) -> p (j m) u e", u=2, e=2),
-                in1=prod[:, 1].rearrange("p j (m u e) -> p (j m) u e", u=2, e=2)[:, :, :, ::-1], op=ALU.add)
-
-        def added_turn(k):
-            g, jp = divmod(k, 2)
-            words = state["d", g][:].bitcast(F32).rearrange("p (u j m) -> p u j m", u=2, j=R)
-            bank = turn_bank("added%d" % k)
-            for jj in range(2):
-                for u in range(2):
-                    nc.tensor.transpose(bank[:, (2 * jj + u) * P:(2 * jj + u + 1) * P], words[:, u, 2 * jp + jj, :], ident[:])
-            state["turn", ("f", g), jp] = bank
-
-        def added_interleave(g, engine):
-            tile = staged("il_t%d" % g)
-            copy_on(engine, tile[:].rearrange("p (u c i j) -> p u c j i", u=2, i=4, j=R), state["d", g][:].rearrange("p (u j c i) -> p u c j i", u=2, j=R, i=4))
-            state["t", g] = tile
-
-        def rotate_turn(k, jj):
-            prod = state["prod", k]
-            bank = turn_bank("rot%d_%d" % (k, jj))
-            for t in range(R):
-                nc.tensor.matmul(bank[:, t * P:(t + 1) * P], lhsT=prod[:, 0, t, jj, :], rhs=ident[:], start=True, stop=False, is_transpose=True)
-                nc.tensor.matmul(bank[:, t * P:(t + 1) * P], lhsT=prod[:, 1, t ^ 1, jj, :], rhs=ident[:], start=False, stop=True, is_transpose=True)
-            state["rot", k, jj] = bank
-
-        def rotate_copy(k, jj, engine="S"):
-            g, jp = divmod(k, 2)
-            j = 2 * jp + jj
-            if j == 0:
-                state["f", g] = staged("f%d" % g)
-            copy_on(engine, state["f", g][:, j * N:(j + 1) * N].rearrange("m (p t) -> m p t", t=R), state["rot", k, jj][:].rearrange("m (t p) -> m p t", t=R))
-
-        def back_turn(g):
-            words = state["f", g][:].bitcast(F32).rearrange("m (j p u) -> m j p u", j=R, u=2)
-            for u in range(2):
-                bank = turn_bank("back%d_%d" % (g, u))
-                for j in range(R):
-                    nc.tensor.transpose(bank[:, j * P:(j + 1) * P], words[:, j, :, u], ident[:])
-                state["back", g, u] = bank
-
-        def back_copy(g, u, engine="S"):
-            if u == 0:
-                state["t", g] = staged("t%d" % g)
-            copy_on(engine, state["t", g][:, u * 2 * N:(u + 1) * 2 * N].rearrange("p (c j) -> p c j", j=R), state["back", g, u][:].bitcast(BF16).rearrange("p (j c) -> p c j", j=R))
-
-        def word_turn(key):
-            if key[0] == "f":
-                words = g_sb[key[1]][:].rearrange("p r c -> p (r c)").bitcast(F32).rearrange("p (r w) -> p r w", r=R)
-            else:
-                h, g = divmod(key[1], 6)
-                words = w_sb[g // 2, h][:].rearrange("p r c -> p (r c)").bitcast(F32).rearrange("p (r w) -> p r w", r=R)[:, :, (g % 2) * 256:(g % 2 + 1) * 256]
-            for half in range(2):
-                bank = turn_bank("turn_%s%d_%d" % (key + (half,)))
-                for rr in range(2):
+                for r in range(2):
                     for u in range(2):
-                        nc.tensor.transpose(bank[:, (2 * rr + u) * P:(2 * rr + u + 1) * P], words[:, 2 * half + rr, u:256:2], ident[:])
-                state["turn", key, half] = bank
+                        nc.tensor.transpose(
+                            banks[h][:, block(2 * r + u)], words[:, 2 * h + r, first_word + u:first_word + N // 2:2],
+                            ident[:])
+            for h in range(2):
+                nc.scalar.copy(
+                    out=dst.bitcast(F32)[:, half(h)].rearrange("m (r p u) -> m r p u", r=2, u=2),
+                    in_=banks[h][:].rearrange("m (r u p) -> m r p u", r=2, u=2))
 
-        def word_copy(key, half, engine="S"):
-            if half == 0:
-                state[key] = staged("st_%s%d" % key)
-            words = state[key][:].bitcast(F32)[:, half * N:(half + 1) * N]
-            copy_on(engine, words.rearrange("m (r p u) -> m r p u", r=2, u=2), state["turn", key, half][:].rearrange("m (r u p) -> m r p u", r=2, u=2))
+        xn_rows = {}
 
-        def dw_mm(i, b, halves=(0, 1)):
-            xc, xs = state["q", ("xn", b // 4)]
-            cols = slice((b % 4) * P, (b % 4 + 1) * P)
-            for gg in halves:
-                zc, zs = state["q", ("t", 2 * i + gg)]
-                bank = (turn_bank if state.get("late") else sum_bank)("dw%d_%d_%d" % (i, b, gg))
-                nc.tensor.matmul_mx(out=bank[:], lhsT=xc[:, cols].bitcast(E4), lhsT_scale=xs[:, cols], rhs=zc[:].bitcast(E5), rhs_scale=zs[:], start=True, stop=True)
-                state["dw", i, b, gg] = bank
+        def make_xn(h):
+            xn_rows[h] = row_tile("xn_rows%d" % h)[:].bitcast(BF16)
+            for j in range(R):
+                nc.vector.scalar_tensor_tensor(
+                    out=xn_rows[h][:, half(j)], in0=x_sb[:, j, half(h)], scalar=inv[:, j:j + 1], in1=lw_bank[h][:],
+                    op0=ALU.mult, op1=ALU.mult)
 
-        def dw_copy(i, b, gg, engine="S"):
-            key = ("dw_rows", i, b)
-            if key not in state:
-                state[key] = ring.tile([P, J], F32, name="dw_rows%d_%d" % (i, b), tag="rows", bufs=7)
-            dst = state[key][:, gg * N:(gg + 1) * N]
-            bank = state["dw", i, b, gg]
-            if i < 2:
-                copy_on(engine, dst.rearrange("p (m u e) -> p m u e", u=2, e=2), bank[:].rearrange("p (u m e) -> p m u e", u=2, e=2))
-            else:
-                copy_on(engine, dst, bank[:])
+        def interleave_xn(h, copy):
+            staged["xn", h] = row_tile("xn_staged%d" % h)[:].bitcast(BF16)
+            interleave(copy, staged["xn", h], xn_rows[h])
 
-        def dw_store(i, b):
-            nc.sync.dma_start(out=dw_out[i][b * P:(b + 1) * P, :], in_=state["dw_rows", i, b][:])
+        dz_rows = {g: grad_sb[g] for g in V_CHUNKS}
+        products = {}
 
-        def dx_mm(h, j, passes):
-            if ("dx", h, j) not in state:
-                state["dx", h, j] = sum_bank("dx%d_%d" % (h, j))
-            cols = slice(j * P, (j + 1) * P)
-            for g in passes:
-                zc, zs = state["q", ("f", g)]
-                wc, ws = state["q", ("w", 6 * h + g)]
-                nc.tensor.matmul_mx(out=state["dx", h, j][:], lhsT=zc[:, cols].bitcast(E5), lhsT_scale=zs[:, cols], rhs=wc[:].bitcast(E4), rhs_scale=ws[:], start=(g == ORDER[0]), stop=(g == ORDER[-1]))
+        def interleave_v(g):
+            staged["dz", g] = gpsimd_tile("dz_staged%d" % g, [P, 2 * CHUNK], BF16)
+            nc.gpsimd.tensor_scalar(
+                out=staged["dz", g][:, CHUNK:2 * CHUNK].rearrange("p (c j) -> p c j", j=R),
+                in0=dz_rows[g].rearrange("p (j c) -> p c j", j=R), scalar1=1.0, scalar2=0.0,
+                op0=ALU.mult, op1=ALU.add)
 
-        part = keep.tile([P, R, 2], F32, name="part")
-        coef = keep.tile([P, R], F32, name="coef")
+        def multiply(g):
+            shape = "p (j h i e) -> p j h i e"
+            rows = grad_sb[g].rearrange(shape, j=R, h=N // HD, e=2)
+            for table, operand in ((SIN, rows[:, :, :, :, ::-1]), (COS, rows)):
+                products[g, table] = wide_tile("product%d_%d" % (g, table))
+                factor = tables[table][:].rearrange("p (j i e) -> p j i e", j=R, e=2).unsqueeze(2)
+                nc.vector.tensor_tensor(
+                    out=products[g, table][:].rearrange(shape, j=R, h=N // HD, e=2), in0=operand,
+                    in1=factor.to_broadcast([P, R, N // HD, HD // 2, 2]), op=ALU.mult)
+
+        def add_products(engine, g, cols):
+            engine.tensor_tensor(
+                out=dz_rows[g][:, cols], in0=products[g, COS][:, cols], in1=products[g, SIN][:, cols], op=ALU.add)
+
+        def turn_dz(g):
+            turn_words("dz%d" % g, dz_rows[g], 0, staged["dz", g][:, :CHUNK])
+
+        def interleave_dz(g):
+            interleave(nc.vector.tensor_copy, staged["dz", g][:, CHUNK:2 * CHUNK], dz_rows[g])
+
+        def turn_weight(i, h, chunk):
+            if chunk == 0:
+                staged["w", i, h] = staging_tile("w_staged%d%d" % (i, h))
+            turn_words("w%d%d%d" % (i, h, chunk), w_sb[i, h][:], chunk * N // 2,
+                       staged["w", i, h][:, chunk * CHUNK:(chunk + 1) * CHUNK])
+
+        def dw_rows(g, pair):
+            xn_codes, xn_scales = mx["xn", pair // 2]
+            dz_codes, dz_scales = mx["dz", g]
+            rows = row_tile("dw%d_%d" % (g, pair))
+            for r in range(2):
+                cols = block(pair % 2 * 2 + r)
+                bank = next_bank("dw%d_%d_%d" % (g, pair, r))
+                nc.tensor.matmul_mx(
+                    out=bank[:], lhsT=xn_codes[:, cols].bitcast(E4), lhsT_scale=xn_scales[:, cols],
+                    rhs=dz_codes[:, N:].bitcast(E5), rhs_scale=dz_scales[:, N:], start=True, stop=True)
+                nc.scalar.copy(out=rows[:, half(r)], in_=bank[:])
+            dst = dw_out[g // 2][2 * pair * P:2 * (pair + 1) * P, half(g % 2)]
+            nc.sync.dma_start(
+                out=dst.rearrange("(r p) c -> p r c", r=2), in_=rows[:].rearrange("p (r c) -> p r c", r=2))
+
+        weight_keys = [("w", i, h) for i in (2, 0, 1) for h in range(2)]
+        weight_jobs = [(turn_weight, key[1:] + (chunk,)) for key in weight_keys for chunk in range(2)]
+        dw_jobs = [(dw_rows, (g, pair)) for g in PASS_ORDER for pair in range(4)]
+        opening = weight_jobs[:2] + [(turn_dz, (V_CHUNKS[1],))] + dw_jobs[:2]
+        alternating = [job for both in zip(weight_jobs[2:], dw_jobs[2:]) for job in both]
+        jobs = opening + alternating + dw_jobs[len(weight_jobs):]
+
+        def side_jobs(count):
+            for run, args in jobs[:count]:
+                run(*args)
+                jobs.remove((run, args))
+
+        dxn = {}
+        gained = {}
+        row_factor = keep.tile([P, R], F32, name="row_factor")
+
+        def dxn_passes(h, j, chunks):
+            for g in chunks:
+                if g == PASS_ORDER[0]:
+                    dxn[h, j] = hold_bank("dxn%d_%d" % (h, j))
+                dz_codes, dz_scales = mx["dz", g]
+                w_codes, w_scales = mx["w", g // 2, h]
+                nc.tensor.matmul_mx(
+                    out=dxn[h, j][:], lhsT=dz_codes[:, block(j)].bitcast(E5), lhsT_scale=dz_scales[:, block(j)],
+                    rhs=w_codes[:, half(g % 2)].bitcast(E4), rhs_scale=w_scales[:, half(g % 2)],
+                    start=(g == PASS_ORDER[0]), stop=(g == PASS_ORDER[-1]))
+
+        def dxn_row(j, chunks):
+            for h in range(2):
+                dxn_passes(h, j, chunks)
 
         def gain(h, j):
-            if h == 0 and j % 2 == 0:
-                state["g", j // 2] = ring.tile([P, 2, D], F32, name="gain%d" % j, tag="prod", bufs=2)
-            cols = slice(h * N, (h + 1) * N)
+            if h == 0:
+                gained[j] = wide_tile("gained%d" % j)
             nc.vector.scalar_tensor_tensor(
-                out=state["g", j // 2][:, j % 2, cols].rearrange("p (q b) -> p q b", b=R),
-                in0=state["dx", h, j][:].rearrange("p (b q) -> p q b", b=R), scalar=iv[:, j:j + 1],
-                in1=lw[:, cols].rearrange("p (q b) -> p q b", b=R), op0=ALU.mult, op1=ALU.mult)
+                out=gained[j][:, half(h)].rearrange("p (q b) -> p q b", b=R),
+                in0=dxn[h, j][:].rearrange("p (b q) -> p q b", b=R), scalar=inv[:, j:j + 1],
+                in1=lw[:, half(h)].rearrange("p (q b) -> p q b", b=R), op0=ALU.mult, op1=ALU.mult)
+            release_bank("dxn%d_%d" % (h, j))
 
-        def row_sum(h, j):
-            cols = slice(h * N, (h + 1) * N)
-            terms = ring.tile([P, N], F32, name="terms%d_%d" % (h, j), tag="rotated", bufs=2)
-            nc.vector.scalar_tensor_tensor(out=terms[:], in0=state["g", j // 2][:, j % 2, cols], scalar=mean_coef[:, j:j + 1], in1=x_sb[:, j, cols], op0=ALU.mult, op1=ALU.mult, accum_out=part[:, j, h:h + 1])
+        def row_sum(j):
+            nc.vector.scalar_tensor_tensor(
+                out=gained[j][:, D:], in0=gained[j][:, :D], scalar=mean_factor[:, j:j + 1], in1=x_sb[:, j, :],
+                op0=ALU.mult, op1=ALU.mult, accum_out=row_factor[:, j:j + 1])
 
-        def join_sum(j):
-            nc.vector.tensor_tensor(out=coef[:, j:j + 1], in0=part[:, j, 0:1], in1=part[:, j, 1:2], op=ALU.add)
+        def finish(j, cols):
+            nc.vector.scalar_tensor_tensor(
+                out=gained[j][:, cols], in0=x_sb[:, j, cols], scalar=row_factor[:, j:j + 1], in1=gained[j][:, cols],
+                op0=ALU.mult, op1=ALU.add)
+            nc.sync.dma_start(
+                out=out_0.rearrange("b (p j) d -> p (b j) d", j=R)[:, j, cols], in_=gained[j][:, cols])
 
-        def finish(j):
-            rows = state["g", j // 2][:, j % 2, :]
-            nc.vector.scalar_tensor_tensor(out=rows, in0=x_sb[:, j, :], scalar=coef[:, j:j + 1], in1=rows, op0=ALU.mult, op1=ALU.add)
-            nc.sync.dma_start(out=out_0.rearrange("b (p j) d -> p (b j) d", j=R)[:, j, :], in_=rows)
+        for h in range(2):
+            spread_lw(h)
+        flip_angles(SIN)
+        flip_angles(COS)
+        make_xn(0)
+        interleave_v(4)
+        turn_dz(4)
+        make_xn(1)
+        flip_back(SIN)
+        flip_back(COS)
+        interleave_xn(0, nc.scalar.copy)
+        interleave_xn(1, nc.vector.tensor_copy)
+        for h in range(2):
+            release_bank("lw%d" % h)
+        quantize(("xn", 0))
+        quantize(("dz", 4))
+        quantize(("xn", 1))
+        interleave_v(5)
+        multiply(0)
+        side_jobs(len(opening))
+        quantize(("dz", 5))
+        side_jobs(2)
 
-        def dw(i, b, engines="SS"):
-            dw_mm(i, b)
-            dw_copy(i, b, 0, engines[0])
-            dw_copy(i, b, 1, engines[1])
-            dw_store(i, b)
+        for g in Q_K_CHUNKS[:-1]:
+            last = g == Q_K_CHUNKS[-2]
+            beside = LAST_JOBS_BESIDE if last else JOBS_BESIDE
+            after = LAST_JOBS_AFTER if last else JOBS_AFTER
+            ready = PASS_ORDER[max(2 * g - 2, 0):2 * g]
+            staged["dz", g] = gpsimd_tile("dz_staged%d" % g, [P, 3 * CHUNK], BF16)
+            dz_rows[g] = staged["dz", g][:, 2 * CHUNK:]
+            add_products(nc.gpsimd, g, slice(0, GPSIMD_COLUMNS))
+            multiply(g + 1)
+            side_jobs(2)
+            dxn_row(0, ready[:1])
+            side_jobs(beside - 2)
+            dxn_row(0, ready[1:])
+            add_products(nc.vector, g, slice(GPSIMD_COLUMNS, CHUNK))
+            if last:
+                release_bank("table%d" % COS)
+                release_bank("table%d" % SIN)
+            turn_dz(g)
+            quantize(weight_keys[2 * g])
+            side_jobs(after // 2)
+            dxn_passes(0, 1, ready)
+            if last:
+                dxn_passes(1, 1, PASS_ORDER[:2 * g])
+            side_jobs(after // 2)
+            interleave_dz(g)
+            quantize(weight_keys[2 * g + 1])
+            quantize(("dz", g))
 
-        def wturn(n, engines="SS"):
-            word_turn(("w", n))
-            word_copy(("w", n), 0, engines[0])
-            word_copy(("w", n), 1, engines[1])
+        before_last, final = Q_K_CHUNKS[-2:]
+        dz_rows[final] = row_tile("dz_rows%d" % final)[:].bitcast(BF16)
+        add_products(nc.vector, final, slice(0, CHUNK))
+        side_jobs(1)
+        dxn_row(0, (before_last,))
+        side_jobs(1)
+        staged["dz", final] = staging_tile("dz_staged%d" % final)
+        turn_dz(final)
+        dxn_row(1, (before_last,))
+        side_jobs(1)
+        interleave_dz(final)
+        quantize(("dz", final), 0, 2 * P)
+        dxn_row(0, (final,))
+        side_jobs(1)
+        quantize(("dz", final), N, N)
+        dxn_row(1, (final,))
+        quantize(("dz", final), 2 * P, 2 * P)
+        side_jobs(1)
 
-        def rot(k):
-            rotate_turn(k, 0)
-            rotate_turn(k, 1)
-            rotate_copy(k, 0)
-            rotate_copy(k, 1)
-
-        def back(g):
-            back_turn(g)
-            back_copy(g, 0)
-            back_copy(g, 1)
-
-        def added(k):
-            added_turn(k)
-            word_copy(("f", k // 2), k % 2)
-
-        def prod(k):
-            product(k, 1)
-            product(k, 0)
-
-        def prod_n(k):
-            product_n(k, 1)
-            product_n(k, 0)
-
-        def half_dw(i, b, gg):
-            dw_mm(i, b, (gg,))
-            dw_copy(i, b, gg)
-            if gg:
-                dw_store(i, b)
-
-        def q(kind, n):
-            quantize((kind, n), E5 if kind in "tf" else E4)
-
-        dws = [(2, b) for b in range(0, 8)] + [(0, b) for b in range(8)] + [(1, b) for b in range(8)]
-        def d(engines="SS"):
-            dw(*dws.pop(0), engines)
-
-        state["late"] = True
-        table(1, True)
-        lw_turn()
-        interleave("V", ("t", 4), g_sb[4][:])
-        lw_copy(0)
-        table(0, True)
-        lw_copy(1)
-        word_turn(("f", 4))
-        xn_rows(0)
-        word_copy(("f", 4), 0)
-        word_copy(("f", 4), 1)
-        q("t", 4)
-        interleave("S", ("xn", 0), state["xn_rows", 0][:])
-        word_turn(("f", 5))
-        word_copy(("f", 5), 0)
-        word_copy(("f", 5), 1)
-        interleave("S", ("t", 5), g_sb[5][:])
-        units = [6 * h + g for g in ORDER for h in range(2)]
-        ready = [("xn", 0)]
-        soon = [("f", 4), ("t", 5)]
-        nd = [0,0, 0,1, 1,1, 1,2, 1,1, 1,1, 1,1, 2,0]
-        nw = [0,0, 1,1, 1,1, 1,1, 1,1, 1,1, 1,1, 0,0]
-        il = "VVVV"
-        passes = [(),(),(),(0,),(),(1,4),(5,),(2,),(3,)]
-
-        def side_work(nunits, njobs, engines="SS"):
-            for n in range(max(nunits, njobs)):
-                if n < nunits:
-                    unit = units.pop(0)
-                    wturn(unit)
-                    soon.append(("w", unit))
-                if n < njobs:
-                    d()
-
-        def flush():
-            for key in ready:
-                q(*key)
-            ready.clear()
-            ready.extend(soon)
-            soon.clear()
-
-        for k in range(8):
-            prod_n(k)
-            if k == 99:
-                state["late"] = True
-            if k:
-                added(k - 1)
-                if k % 2 == 0:
-                    soon.append(("f", k // 2 - 1))
-                    if il[k // 2 - 1] == "S":
-                        added_interleave(k // 2 - 1, "S")
-                        soon.append(("t", k // 2 - 1))
-            side_work(nw[2 * k], nd[2 * k])
-            flush()
-            rotate_add(k)
-            if k == 0:
-                xn_rows(1)
-                interleave("S", ("xn", 1), state["xn_rows", 1][:])
-                soon.extend([("xn", 1), ("f", 5)])
-            for g in passes[k]:
-                for j in range(2):
-                    for h in range(2):
-                        dx_mm(h, j, (g,))
-            side_work(nw[2 * k + 1], nd[2 * k + 1])
-            flush()
-            if k % 2 == 1 and il[k // 2] == "V":
-                added_interleave(k // 2, "V")
-                ready.append(("t", k // 2))
-        added(7)
-        side_work(0, 2)
-        q("f", 3)
-        flush()
-        flush()
-        for j in range(2):
-            for h in range(2):
-                dx_mm(h, j, passes[8])
-        tail = ["xd","xddxd","xdd",""]
-        later = [(h, j) for j in (2, 3) for h in range(2)]
-        d()
-        d()
-        for j in range(4):
-            gain(0, j)
-            if j:
-                join_sum(j - 1)
-            gain(1, j)
-            if j:
-                finish(j - 1)
-            for c in tail[j]:
-                if c == "d":
-                    d()
-                else:
-                    dx_mm(*later.pop(0), ORDER)
-            row_sum(0, j)
-            row_sum(1, j)
-        join_sum(3)
-        finish(3)
-        assert not dws
+        gain(0, 0)
+        gain(1, 0)
+        dxn_passes(0, 2, PASS_ORDER)
+        side_jobs(1)
+        dxn_passes(1, 2, PASS_ORDER)
+        last_row_halves = [0, 1]
+        for j in range(R - 1):
+            gain(0, j + 1)
+            row_sum(j)
+            gain(1, j + 1)
+            finish(j, slice(0, D))
+            side_jobs(1)
+            if last_row_halves:
+                dxn_passes(last_row_halves.pop(0), R - 1, PASS_ORDER)
+        row_sum(R - 1)
+        for h in range(2):
+            finish(R - 1, half(h))
+        assert not jobs

import math
from contextlib import ExitStack

import concourse.mybir as mybir
from concourse.masks import make_identity

T, D, J = 512, 1024, 1024
HD = 128
THETA = 10000.0
FLOPS = 2 * 2 * T * D * 3 * J

F32 = mybir.dt.float32
BF16 = mybir.dt.bfloat16
I32 = mybir.dt.int32
U32 = mybir.dt.uint32
U8 = mybir.dt.uint8
E4 = mybir.dt.float8_e4m3fn_x4
E5 = mybir.dt.float8_e5m2_x4
ALU = mybir.AluOpType
ACT = mybir.ActivationFunctionType

P = 128
R = 4
N = 512
CHUNK = R * N
PAIRS = R * HD // 2
BANKS = 8
Q_K_CHUNKS = (0, 1, 2, 3)
V_CHUNKS = (4, 5)
PASS_ORDER = V_CHUNKS + Q_K_CHUNKS
COS, SIN = 0, 1

GPSIMD_COLUMNS = 1664
JOBS_BESIDE, JOBS_AFTER = 4, 4
LAST_JOBS_BESIDE, LAST_JOBS_AFTER = 3, 2
ROW_TILES = 7
WIDE_TILES = 4
STAGING_TILES = 3


def tile_pagedllamablock_pa_v_kernel(
    tc, x, ln_w, wq, wk, wv, inv_rms, grad_0, grad_1, grad_2, out_0, out_1, out_2, out_3
):
    nc = tc.nc
    weights = (wq, wk, wv)
    grads = (grad_0, grad_1, grad_2)
    dw_out = (out_1, out_2, out_3)

    with ExitStack() as ctx:
        keep = ctx.enter_context(tc.tile_pool(name="keep", bufs=1))
        ring = ctx.enter_context(tc.tile_pool(name="ring", bufs=1))
        psum = ctx.enter_context(tc.psum_pool(name="psum", bufs=1))
        ctx.enter_context(tc.manual_schedule())

        rotation = list(range(BANKS))
        held = {}

        def next_bank(name):
            number = rotation.pop(0)
            rotation.append(number)
            return psum.tile([P, N], F32, name=name, tag="bank%d" % number)

        def hold_bank(name):
            held[name] = rotation.pop(0)
            return psum.tile([P, N], F32, name=name, tag="bank%d" % held[name])

        def release_bank(name):
            rotation.append(held[name])

        def row_tile(name):
            return ring.tile([P, J], F32, name=name, tag="rows", bufs=ROW_TILES, align_bytes=64)

        def wide_tile(name):
            return ring.tile([P, CHUNK], F32, name=name, tag="wide", bufs=WIDE_TILES)

        def staging_tile(name):
            return ring.tile([P, 2 * CHUNK], BF16, name=name, tag="staging", bufs=STAGING_TILES, align_bytes=64)

        def gpsimd_tile(name, shape, dtype):
            return ring.tile(shape, dtype, name=name, tag="gpsimd", bufs=1, align_bytes=64)

        def by_row(ap):
            return ap.rearrange("p (r c) -> p r c", r=R)

        def half(h):
            return slice(h * N, (h + 1) * N)

        def block(b):
            return slice(b * P, (b + 1) * P)

        inv = keep.tile([P, R], F32, name="inv")
        lw_cols = keep.tile([P, 2, R], BF16, name="lw_cols")
        x_sb = keep.tile([P, R, D], BF16, name="x_sb")
        v_rows = wide_tile("v_rows")[:].bitcast(BF16)
        grad_sb = [keep.tile([P, CHUNK], BF16, name="grad%d" % g)[:] for g in Q_K_CHUNKS]
        grad_sb.extend([v_rows[:, :CHUNK], v_rows[:, CHUNK:]])
        w_sb = {(i, h): keep.tile([P, R * J], BF16, name="w%d%d" % (i, h)) for i in range(3) for h in range(2)}

        def load_grad(g):
            rows = grads[g // 2].rearrange("b (p j) h e -> p (b j) (h e)", j=R)
            nc.sync.dma_start(out=by_row(grad_sb[g]), in_=rows[:, :, half(g % 2)])

        def load_x(h):
            rows = x.rearrange("b (p j) d -> p (b j) d", j=R)
            nc.sync.dma_start(out=x_sb[:, :, half(h)], in_=rows[:, :, half(h)])

        def load_w(i, h):
            nc.sync.dma_start(out=w_sb[i, h][:], in_=weights[i][half(h), :].rearrange("(p b) c -> p (b c)", b=R))

        nc.sync.dma_start(out=lw_cols[:], in_=ln_w.rearrange("(h p b) -> p h b", h=2, b=R))
        nc.sync.dma_start(out=inv[:], in_=inv_rms.rearrange("b (p j) o -> p (b j o)", j=R))
        load_x(0)
        load_grad(4)
        load_x(1)
        load_w(2, 0)
        load_grad(5)
        load_grad(0)
        load_w(2, 1)
        load_grad(1)
        load_w(0, 0)
        load_w(0, 1)
        load_grad(2)
        load_w(1, 0)
        load_w(1, 1)
        load_grad(3)

        position = keep.tile([P, R], I32, name="position")
        nc.gpsimd.iota(position[:], pattern=[[1, R]], base=0, channel_multiplier=R)
        ident = keep.tile([P, P], F32, name="ident")
        make_identity(nc, ident[:])

        scratch = row_tile("angle_scratch")
        turns = scratch[:, :PAIRS]
        whole_turns = scratch[:, PAIRS:2 * PAIRS].bitcast(I32)
        by_frequency = turns.rearrange("p (j a b) -> p j a b", j=R, a=8)
        for b in range(8):
            nc.vector.tensor_scalar(
                out=by_frequency[:, :, 0, b], in0=position[:], scalar1=THETA ** (-b / 64) / (2 * math.pi),
                scalar2=None, op0=ALU.mult)
        for a in range(1, 8):
            nc.vector.tensor_scalar(
                out=by_frequency[:, :, a, :], in0=by_frequency[:, :, 0, :], scalar1=THETA ** (-a / 8),
                scalar2=None, op0=ALU.mult)
        lw_f32 = keep.tile([P, 2, R], F32, name="lw_f32")
        nc.vector.tensor_copy(out=lw_f32[:], in_=lw_cols[:])
        nc.vector.tensor_copy(out=whole_turns, in_=turns)
        mean_factor = keep.tile([P, R], F32, name="mean_factor")
        nc.vector.scalar_tensor_tensor(
            out=mean_factor[:], in0=inv[:], scalar=-1.0 / D, in1=inv[:], op0=ALU.mult, op1=ALU.mult)
        angles = gpsimd_tile("angles", [P, 2 * N], F32)
        signed = angles[:, half(SIN)].rearrange("p (i e) -> p i e", e=2)
        nc.vector.tensor_tensor(out=signed[:, :, 0], in0=turns, in1=whole_turns, op=ALU.subtract)
        nc.vector.tensor_tensor(out=signed[:, :, 1], in0=whole_turns, in1=turns, op=ALU.subtract)
        nc.vector.tensor_tensor(
            out=angles[:, half(COS)].rearrange("p (i e) -> p i e", e=2), in0=signed, in1=signed[:, :, ::-1],
            op=ALU.min)

        flipped = row_tile("flipped_tables")
        tables = {}

        def flip_angles(table):
            bank = next_bank("flipped_angles%d" % table)
            for j in range(R):
                nc.tensor.transpose(bank[:, block(j)], angles[:, half(table)][:, block(j)], ident[:])
            nc.scalar.activation(
                out=flipped[:, half(table)], in_=bank[:], func=ACT.Sin, scale=2 * math.pi,
                bias=math.pi / 2 if table == COS else 0.0)

        def flip_back(table):
            tables[table] = hold_bank("table%d" % table)
            for j in range(R):
                nc.tensor.transpose(tables[table][:, block(j)], flipped[:, half(table)][:, block(j)], ident[:])

        lw = keep.tile([P, D], F32, name="lw")
        lw_bank = {}

        def spread_lw(h):
            lw_bank[h] = hold_bank("lw%d" % h)
            for b in range(R):
                nc.tensor.transpose(lw_bank[h][:, b:N:R], lw_f32[:, h, b:b + 1].to_broadcast([P, P]), ident[:])
            nc.scalar.copy(out=lw[:, half(h)], in_=lw_bank[h][:])

        staged = {}
        mx = {}

        def quantize(key, first=0, width=None):
            total = N if key[0] == "xn" else 2 * N
            width = width or total
            if key not in mx:
                name = "_".join(map(str, key))
                codes = keep.tile([P, total], U32, name=name + "_codes", align_bytes=64)
                scales = keep.tile([P, total], U8, name=name + "_scales", align_bytes=64)
                mx[key] = (codes, scales)
            codes, scales = mx[key]
            cols = slice(first, first + width)
            nc.vector.quantize_mx(
                out=codes[:, cols].bitcast(E5 if key[0] == "dz" else E4), scales=scales[:, cols],
                in_=staged[key][:, R * first:R * (first + width)])

        def interleave(copy, dst, rows):
            copy(out=dst.rearrange("p (c i j) -> p c j i", i=4, j=R),
                 in_=rows.rearrange("p (j c i) -> p c j i", j=R, i=4))

        def turn_words(name, rows, first_word, dst):
            words = by_row(rows.bitcast(F32))
            banks = [next_bank("%s_%d" % (name, h)) for h in range(2)]
            for h in range(2):
                for r in range(2):
                    for u in range(2):
                        nc.tensor.transpose(
                            banks[h][:, block(2 * r + u)], words[:, 2 * h + r, first_word + u:first_word + N // 2:2],
                            ident[:])
            for h in range(2):
                nc.scalar.copy(
                    out=dst.bitcast(F32)[:, half(h)].rearrange("m (r p u) -> m r p u", r=2, u=2),
                    in_=banks[h][:].rearrange("m (r u p) -> m r p u", r=2, u=2))

        xn_rows = {}

        def make_xn(h):
            xn_rows[h] = row_tile("xn_rows%d" % h)[:].bitcast(BF16)
            for j in range(R):
                nc.vector.scalar_tensor_tensor(
                    out=xn_rows[h][:, half(j)], in0=x_sb[:, j, half(h)], scalar=inv[:, j:j + 1], in1=lw_bank[h][:],
                    op0=ALU.mult, op1=ALU.mult)

        def interleave_xn(h, copy):
            staged["xn", h] = row_tile("xn_staged%d" % h)[:].bitcast(BF16)
            interleave(copy, staged["xn", h], xn_rows[h])

        dz_rows = {g: grad_sb[g] for g in V_CHUNKS}
        products = {}

        def interleave_v(g):
            staged["dz", g] = gpsimd_tile("dz_staged%d" % g, [P, 2 * CHUNK], BF16)
            nc.gpsimd.tensor_scalar(
                out=staged["dz", g][:, CHUNK:2 * CHUNK].rearrange("p (c j) -> p c j", j=R),
                in0=dz_rows[g].rearrange("p (j c) -> p c j", j=R), scalar1=1.0, scalar2=0.0,
                op0=ALU.mult, op1=ALU.add)

        def multiply(g):
            shape = "p (j h i e) -> p j h i e"
            rows = grad_sb[g].rearrange(shape, j=R, h=N // HD, e=2)
            for table, operand in ((SIN, rows[:, :, :, :, ::-1]), (COS, rows)):
                products[g, table] = wide_tile("product%d_%d" % (g, table))
                factor = tables[table][:].rearrange("p (j i e) -> p j i e", j=R, e=2).unsqueeze(2)
                nc.vector.tensor_tensor(
                    out=products[g, table][:].rearrange(shape, j=R, h=N // HD, e=2), in0=operand,
                    in1=factor.to_broadcast([P, R, N // HD, HD // 2, 2]), op=ALU.mult)

        def add_products(engine, g, cols):
            engine.tensor_tensor(
                out=dz_rows[g][:, cols], in0=products[g, COS][:, cols], in1=products[g, SIN][:, cols], op=ALU.add)

        def turn_dz(g):
            turn_words("dz%d" % g, dz_rows[g], 0, staged["dz", g][:, :CHUNK])

        def interleave_dz(g):
            interleave(nc.vector.tensor_copy, staged["dz", g][:, CHUNK:2 * CHUNK], dz_rows[g])

        def turn_weight(i, h, chunk):
            if chunk == 0:
                staged["w", i, h] = staging_tile("w_staged%d%d" % (i, h))
            turn_words("w%d%d%d" % (i, h, chunk), w_sb[i, h][:], chunk * N // 2,
                       staged["w", i, h][:, chunk * CHUNK:(chunk + 1) * CHUNK])

        def dw_rows(g, pair):
            xn_codes, xn_scales = mx["xn", pair // 2]
            dz_codes, dz_scales = mx["dz", g]
            rows = row_tile("dw%d_%d" % (g, pair))
            for r in range(2):
                cols = block(pair % 2 * 2 + r)
                bank = next_bank("dw%d_%d_%d" % (g, pair, r))
                nc.tensor.matmul_mx(
                    out=bank[:], lhsT=xn_codes[:, cols].bitcast(E4), lhsT_scale=xn_scales[:, cols],
                    rhs=dz_codes[:, N:].bitcast(E5), rhs_scale=dz_scales[:, N:], start=True, stop=True)
                nc.scalar.copy(out=rows[:, half(r)], in_=bank[:])
            dst = dw_out[g // 2][2 * pair * P:2 * (pair + 1) * P, half(g % 2)]
            nc.sync.dma_start(
                out=dst.rearrange("(r p) c -> p r c", r=2), in_=rows[:].rearrange("p (r c) -> p r c", r=2))

        weight_keys = [("w", i, h) for i in (2, 0, 1) for h in range(2)]
        weight_jobs = [(turn_weight, key[1:] + (chunk,)) for key in weight_keys for chunk in range(2)]
        dw_jobs = [(dw_rows, (g, pair)) for g in PASS_ORDER for pair in range(4)]
        opening = weight_jobs[:2] + [(turn_dz, (V_CHUNKS[1],))] + dw_jobs[:2]
        alternating = [job for both in zip(weight_jobs[2:], dw_jobs[2:]) for job in both]
        jobs = opening + alternating + dw_jobs[len(weight_jobs):]

        def side_jobs(count):
            for run, args in jobs[:count]:
                run(*args)
                jobs.remove((run, args))

        dxn = {}
        gained = {}
        row_factor = keep.tile([P, R], F32, name="row_factor")

        def dxn_passes(h, j, chunks):
            for g in chunks:
                if g == PASS_ORDER[0]:
                    dxn[h, j] = hold_bank("dxn%d_%d" % (h, j))
                dz_codes, dz_scales = mx["dz", g]
                w_codes, w_scales = mx["w", g // 2, h]
                nc.tensor.matmul_mx(
                    out=dxn[h, j][:], lhsT=dz_codes[:, block(j)].bitcast(E5), lhsT_scale=dz_scales[:, block(j)],
                    rhs=w_codes[:, half(g % 2)].bitcast(E4), rhs_scale=w_scales[:, half(g % 2)],
                    start=(g == PASS_ORDER[0]), stop=(g == PASS_ORDER[-1]))

        def dxn_row(j, chunks):
            for h in range(2):
                dxn_passes(h, j, chunks)

        def gain(h, j):
            if h == 0:
                gained[j] = wide_tile("gained%d" % j)
            nc.vector.scalar_tensor_tensor(
                out=gained[j][:, half(h)].rearrange("p (q b) -> p q b", b=R),
                in0=dxn[h, j][:].rearrange("p (b q) -> p q b", b=R), scalar=inv[:, j:j + 1],
                in1=lw[:, half(h)].rearrange("p (q b) -> p q b", b=R), op0=ALU.mult, op1=ALU.mult)
            release_bank("dxn%d_%d" % (h, j))

        def row_sum(j):
            nc.vector.scalar_tensor_tensor(
                out=gained[j][:, D:], in0=gained[j][:, :D], scalar=mean_factor[:, j:j + 1], in1=x_sb[:, j, :],
                op0=ALU.mult, op1=ALU.mult, accum_out=row_factor[:, j:j + 1])

        def finish(j, cols):
            nc.vector.scalar_tensor_tensor(
                out=gained[j][:, cols], in0=x_sb[:, j, cols], scalar=row_factor[:, j:j + 1], in1=gained[j][:, cols],
                op0=ALU.mult, op1=ALU.add)
            nc.sync.dma_start(
                out=out_0.rearrange("b (p j) d -> p (b j) d", j=R)[:, j, cols], in_=gained[j][:, cols])

        for h in range(2):
            spread_lw(h)
        flip_angles(SIN)
        flip_angles(COS)
        make_xn(0)
        interleave_v(4)
        turn_dz(4)
        make_xn(1)
        flip_back(SIN)
        flip_back(COS)
        interleave_xn(0, nc.scalar.copy)
        interleave_xn(1, nc.vector.tensor_copy)
        for h in range(2):
            release_bank("lw%d" % h)
        quantize(("xn", 0))
        quantize(("dz", 4))
        quantize(("xn", 1))
        interleave_v(5)
        multiply(0)
        side_jobs(len(opening))
        quantize(("dz", 5))
        side_jobs(2)

        for g in Q_K_CHUNKS[:-1]:
            last = g == Q_K_CHUNKS[-2]
            beside = LAST_JOBS_BESIDE if last else JOBS_BESIDE
            after = LAST_JOBS_AFTER if last else JOBS_AFTER
            ready = PASS_ORDER[max(2 * g - 2, 0):2 * g]
            staged["dz", g] = gpsimd_tile("dz_staged%d" % g, [P, 3 * CHUNK], BF16)
            dz_rows[g] = staged["dz", g][:, 2 * CHUNK:]
            add_products(nc.gpsimd, g, slice(0, GPSIMD_COLUMNS))
            multiply(g + 1)
            side_jobs(2)
            dxn_row(0, ready[:1])
            side_jobs(beside - 2)
            dxn_row(0, ready[1:])
            add_products(nc.vector, g, slice(GPSIMD_COLUMNS, CHUNK))
            if last:
                release_bank("table%d" % COS)
                release_bank("table%d" % SIN)
            turn_dz(g)
            quantize(weight_keys[2 * g])
            side_jobs(after // 2)
            dxn_passes(0, 1, ready)
            if last:
                dxn_passes(1, 1, PASS_ORDER[:2 * g])
            side_jobs(after // 2)
            interleave_dz(g)
            quantize(weight_keys[2 * g + 1])
            quantize(("dz", g))

        before_last, final = Q_K_CHUNKS[-2:]
        dz_rows[final] = row_tile("dz_rows%d" % final)[:].bitcast(BF16)
        add_products(nc.vector, final, slice(0, CHUNK))
        side_jobs(1)
        dxn_row(0, (before_last,))
        side_jobs(1)
        staged["dz", final] = staging_tile("dz_staged%d" % final)
        turn_dz(final)
        dxn_row(1, (before_last,))
        side_jobs(1)
        interleave_dz(final)
        quantize(("dz", final), 0, 2 * P)
        dxn_row(0, (final,))
        side_jobs(1)
        quantize(("dz", final), N, N)
        dxn_row(1, (final,))
        quantize(("dz", final), 2 * P, 2 * P)
        side_jobs(1)

        gain(0, 0)
        gain(1, 0)
        dxn_passes(0, 2, PASS_ORDER)
        side_jobs(1)
        dxn_passes(1, 2, PASS_ORDER)
        last_row_halves = [0, 1]
        for j in range(R - 1):
            gain(0, j + 1)
            row_sum(j)
            gain(1, j + 1)
            finish(j, slice(0, D))
            side_jobs(1)
            if last_row_halves:
                dxn_passes(last_row_halves.pop(0), R - 1, PASS_ORDER)
        row_sum(R - 1)
        for h in range(2):
            finish(R - 1, half(h))
        assert not jobs
